import numpy as np
import ml_dtypes


def mxq(x, axis, fmt="e4m3"):
    dtype, down = {"e4m3": (ml_dtypes.float8_e4m3fn, 7), "e5m2": (ml_dtypes.float8_e5m2, 14)}[fmt]
    v = np.moveaxis(np.asarray(x, np.float32).astype(ml_dtypes.bfloat16).astype(np.float64), axis, -1)
    blocks = v.reshape(v.shape[:-1] + (-1, 32))
    amax = np.abs(blocks).max(-1, keepdims=True)
    byte = np.maximum(np.where(amax > 0, np.frexp(amax)[1] - 1 + 127, 0) - down, 1)
    scale = np.exp2(byte - 127.0)
    codes = (blocks / scale).astype(np.float32).astype(dtype).astype(np.float64)
    return np.moveaxis((codes * scale).reshape(v.shape), -1, axis)


WIDE = False


def mx_kscale(k):
    if not WIDE:
        return np.ones(k)
    levels = np.array([10, -10, 5, -5, 0])
    a = np.random.permutation(np.resize(levels, k // 512 * 4)).reshape(k // 512, 4)
    idx = np.arange(k)
    return np.exp2(a[idx // 512, idx % 128 // 32])


BF16 = ml_dtypes.bfloat16


def bf(x):
    return np.asarray(x, np.float32).astype(BF16)


def f64(x):
    return np.asarray(x).astype(np.float64)


E2M1 = np.array([0.0, 0.5, 1.0, 1.5, 2.0, 3.0, 4.0, 6.0, -0.0, -0.5, -1.0, -1.5, -2.0, -3.0, -4.0, -6.0])


def pack_weight(w, fmt):
    k, n = w.shape
    w = f64(bf(w)).reshape(k // 32, 32, n)
    amax = np.abs(w).max(1)
    if fmt == "e4m3":
        byte = np.frexp(amax)[1] - 1 + 127 - 7
    else:
        mant, ex = np.frexp(amax / 6.0)
        byte = np.where(mant > 0.5, ex, ex - 1) + 127
    byte = np.clip(np.where(amax > 0, byte, 1), 1, 254)
    scaled = (w * np.exp2(127.0 - byte)[:, None, :]).reshape(k, n).astype(np.float32)
    by_word = np.ascontiguousarray(scaled.reshape(k // 512, 128, 4, n).transpose(0, 1, 3, 2))
    if fmt == "e4m3":
        words = by_word.astype(ml_dtypes.float8_e4m3fn).view(np.uint8)
    else:
        c = by_word.astype(ml_dtypes.float4_e2m1fn).view(np.uint8) & 0xF
        words = c[..., 0::2] | (c[..., 1::2] << 4)
    return np.ascontiguousarray(words), np.ascontiguousarray(byte.astype(np.uint8).reshape(k // 512, 16, n))


def unpack_weight(words, scales, fmt):
    g, p, n, _ = words.shape
    if fmt == "e4m3":
        vals = np.ascontiguousarray(words).view(ml_dtypes.float8_e4m3fn).astype(np.float64)
    else:
        nib = np.empty((g, p, n, 4), np.uint8)
        nib[..., 0::2] = words & 0xF
        nib[..., 1::2] = words >> 4
        vals = E2M1[nib]
    vals = vals * np.repeat(np.exp2(scales.astype(np.float64) - 127.0), 8, axis=1)[..., None]
    return vals.transpose(0, 1, 3, 2).reshape(g * 512, n)


B, H, W, C, UP = 1, 8, 8, 8192, 2
K = C // UP


def setup_inputs():
    s = mx_kscale(K)
    x = bf(np.random.standard_normal((B, H * W, C)) * np.tile(s, UP))
    words, scales = pack_weight(np.random.standard_normal((K, K)) / np.sqrt(K) / s[:, None], "e4m3")
    return {"x": x, "w_words": words, "w_scales": scales}


def reference(x, w_words, w_scales):
    xg = f64(x).reshape(B, H, W, C)
    x0 = xg[..., :K]
    x1 = xg[..., K:]
    xi = np.stack([x0, x1], axis=2).reshape(B, UP * H, W, K)
    y = mxq(xi, 3, "e4m3") @ unpack_weight(w_words, w_scales, "e4m3")
    return y.reshape(B, H * W * UP, K)

@@ -1,0 +1,128 @@
+import concourse.mybir as mybir
+from concourse.masks import make_identity
+
+F32 = mybir.dt.float32
+BF16 = mybir.dt.bfloat16
+I32 = mybir.dt.int32
+U32 = mybir.dt.uint32
+U8 = mybir.dt.uint8
+FP8X4 = mybir.dt.float8_e4m3fn_x4
+
+P = 128
+K = 4096
+N = 4096
+PASSES = K // 512
+BANK = 512
+NBANKS = N // BANK
+FLOPS = 2 * P * K * N
+
+LAST = [(0, 2), (2, 2), (4, 2), (6, 1), (7, 1)]
+
+
+def tile_patch_expanding_w_kernel(tc, x, w_words, w_scales, out):
+    nc = tc.nc
+    x_rows = x.rearrange("b t (r k) -> (b t r) k", r=2)
+    out_rows = out.rearrange("b m n -> (b m) n")
+
+    with tc.tile_pool(name="keep", bufs=1) as keep, tc.psum_pool(
+        name="banks", bufs=1
+    ) as banks, tc.manual_schedule():
+        x_sb = keep.tile([P, K], BF16, name="x_sb", align_bytes=64)
+        nc.sync.dma_start(out=x_sb[:], in_=x_rows)
+
+        planes = keep.tile([P, 2, N], U8, name="planes", align_bytes=64)
+        nc.vector.memset(planes[:].rearrange("p h n -> p (h n)").bitcast(I32), 0)
+
+        ident = keep.tile([P, P], F32, name="ident")
+        make_identity(nc, ident[:])
+        perm = keep.tile([P, P], F32, name="perm")
+        nc.vector.tensor_copy(
+            out=perm[:].rearrange("p (i r j) -> p i r j", i=8, r=2, j=8),
+            in_=ident[:].rearrange("p (i j r) -> p i r j", i=8, j=8, r=2),
+        )
+
+        for h in range(2):
+            for q in range(4):
+                nc.sync.dma_start(
+                    out=planes[32 * q : 32 * q + 16, h, :].bitcast(I32),
+                    in_=w_scales[4 * h : 4 * h + 4, 4 * q : 4 * q + 4, :].bitcast(I32),
+                )
+
+        pieces = []
+        for g in range(PASSES):
+            cuts = LAST if g == PASSES - 1 else [(0, NBANKS)]
+            flat = w_words[g].rearrange("p n t -> p (n t)")
+            row = []
+            for first, count in cuts:
+                wt = keep.tile(
+                    [P, count * BANK * 4], U8, name="w%d_%d" % (g, first), align_bytes=64
+                )
+                nc.sync.dma_start(
+                    out=wt[:].bitcast(I32),
+                    in_=flat[:, first * BANK * 4 : (first + count) * BANK * 4].bitcast(I32),
+                )
+                for b in range(count):
+                    row.append(wt[:, b * BANK * 4 : (b + 1) * BANK * 4])
+            pieces.append(row)
+
+        grouped = keep.tile([P, K], BF16, name="grouped", align_bytes=64)
+        xq = keep.tile([P, PASSES * P], U32, name="xq", align_bytes=64)
+        xs = keep.tile([P, PASSES * P], U8, name="xs", align_bytes=64)
+        xw = x_sb[:].bitcast(F32)
+        gw = grouped[:].bitcast(F32)
+        for b in range(4):
+            tp = banks.tile([P, 4, P], F32, name="tp%d" % b, tag="bank%d" % b)
+            for s in range(4):
+                g = 2 * b + s // 2
+                u = s % 2
+                nc.tensor.transpose(
+                    tp[:, s, :], xw[:, 256 * g + u : 256 * (g + 1) : 2], perm[:]
+                )
+            dst = gw[:, 512 * b : 512 * (b + 1)].rearrange(
+                "p (gl m u) -> p gl m u", gl=2, m=P, u=2
+            )
+            src = tp[:].rearrange("p (gl u) m -> p gl m u", gl=2, u=2)
+            if b % 2 == 0:
+                nc.vector.tensor_copy(out=dst, in_=src)
+            else:
+                nc.scalar.copy(out=dst, in_=src)
+        for hh in range(2):
+            nc.vector.quantize_mx(
+                out=xq[:, 512 * hh : 512 * (hh + 1)].bitcast(FP8X4),
+                scales=xs[:, 512 * hh : 512 * (hh + 1)],
+                in_=grouped[:, 2048 * hh : 2048 * (hh + 1)],
+            )
+
+        acc = []
+        for j in range(NBANKS):
+            acc_j = banks.tile([P, BANK], F32, name="acc%d" % j, tag="bank%d" % j)
+            acc.append(acc_j)
+
+        def one_pass(g, j):
+            k = 4 * (g % 4)
+            nc.tensor.matmul_mx(
+                out=acc[j][:],
+                lhsT=xq[:, P * g : P * (g + 1)].bitcast(FP8X4),
+                lhsT_scale=xs[:, P * g : P * (g + 1)],
+                rhs=pieces[g][j].bitcast(FP8X4),
+                rhs_scale=planes[k:P, g // 4, BANK * j : BANK * (j + 1)],
+                start=(g == 0),
+                stop=(g == PASSES - 1),
+            )
+
+        for g in range(PASSES - 1):
+            for j in range(NBANKS):
+                one_pass(g, j)
+
+        for first, count in LAST:
+            res = keep.tile([P, count * BANK], F32, name="res%d" % first)
+            for b in range(count):
+                j = first + b
+                one_pass(PASSES - 1, j)
+                if j % 2 == 0:
+                    nc.vector.tensor_copy(out=res[:, BANK * b : BANK * (b + 1)], in_=acc[j][:])
+                else:
+                    nc.scalar.copy(out=res[:, BANK * b : BANK * (b + 1)], in_=acc[j][:])
+            nc.sync.dma_start(
+                out=out_rows[:, BANK * first : BANK * (first + count)], in_=res[:]
+            )

@@ -43,9 +43,9 @@ def tile_patch_expanding_w_kernel(tc, x, w_words, w_scales, out):
 
         for h in range(2):
             for q in range(4):
-                nc.sync.dma_start(
-                    out=planes[32 * q : 32 * q + 16, h, :].bitcast(I32),
-                    in_=w_scales[4 * h : 4 * h + 4, 4 * q : 4 * q + 4, :].bitcast(I32),
+                nc.gpsimd.dma_start(
+                    out=planes[32 * q : 32 * q + 16, h, :].bitcast(F32),
+                    in_=w_scales[4 * h : 4 * h + 4, 4 * q : 4 * q + 4, :].bitcast(F32),
                 )
 
         pieces = []

@@ -41,12 +41,15 @@ def tile_patch_expanding_w_kernel(tc, x, w_words, w_scales, out):
             in_=ident[:].rearrange("p (i j r) -> p i r j", i=8, j=8, r=2),
         )
 
-        for h in range(2):
-            for q in range(4):
-                nc.gpsimd.dma_start(
-                    out=planes[32 * q : 32 * q + 16, h, :].bitcast(F32),
-                    in_=w_scales[4 * h : 4 * h + 4, 4 * q : 4 * q + 4, :].bitcast(F32),
-                )
+        for q in (2, 3, 0, 1):
+            for h in range(2):
+                for c in range(0, N, N // 2):
+                    nc.sync.dma_start(
+                        out=planes[32 * q : 32 * q + 16, h, c : c + N // 2].bitcast(I32),
+                        in_=w_scales[
+                            4 * h : 4 * h + 4, 4 * q : 4 * q + 4, c : c + N // 2
+                        ].bitcast(I32),
+                    )
 
         pieces = []
         for g in range(PASSES):

@@ -16,7 +16,9 @@ BANK = 512
 NBANKS = N // BANK
 FLOPS = 2 * P * K * N
 
-LAST = [(0, 2), (2, 2), (4, 2), (6, 1), (7, 1)]
+WHOLE = PASSES - 2
+PIECES = [(0, 4), (4, 2), (6, 1), (7, 1)]
+STORES = [(0, 2), (2, 2), (4, 2), (6, 1), (7, 1)]
 
 
 def tile_patch_expanding_w_kernel(tc, x, w_words, w_scales, out):
@@ -41,32 +43,32 @@ def tile_patch_expanding_w_kernel(tc, x, w_words, w_scales, out):
             in_=ident[:].rearrange("p (i j r) -> p i r j", i=8, j=8, r=2),
         )
 
-        for q in (2, 3, 0, 1):
-            for h in range(2):
-                for c in range(0, N, N // 2):
-                    nc.sync.dma_start(
-                        out=planes[32 * q : 32 * q + 16, h, c : c + N // 2].bitcast(I32),
-                        in_=w_scales[
-                            4 * h : 4 * h + 4, 4 * q : 4 * q + 4, c : c + N // 2
-                        ].bitcast(I32),
-                    )
-
-        pieces = []
-        for g in range(PASSES):
-            cuts = LAST if g == PASSES - 1 else [(0, NBANKS)]
-            flat = w_words[g].rearrange("p n t -> p (n t)")
-            row = []
-            for first, count in cuts:
-                wt = keep.tile(
-                    [P, count * BANK * 4], U8, name="w%d_%d" % (g, first), align_bytes=64
-                )
+        for h in range(2):
+            for q in range(4):
                 nc.sync.dma_start(
-                    out=wt[:].bitcast(I32),
-                    in_=flat[:, first * BANK * 4 : (first + count) * BANK * 4].bitcast(I32),
+                    out=planes[32 * q : 32 * q + 16, h, :].bitcast(I32),
+                    in_=w_scales[4 * h : 4 * h + 4, 4 * q : 4 * q + 4, :].bitcast(I32),
                 )
-                for b in range(count):
-                    row.append(wt[:, b * BANK * 4 : (b + 1) * BANK * 4])
-            pieces.append(row)
+
+        rhs = {}
+
+        def load_words(g, first, count):
+            wt = keep.tile(
+                [P, count * BANK * 4], U8, name="w%d_%d" % (g, first), align_bytes=64
+            )
+            flat = w_words[g].rearrange("p n t -> p (n t)")
+            nc.sync.dma_start(
+                out=wt[:].bitcast(I32),
+                in_=flat[:, first * BANK * 4 : (first + count) * BANK * 4].bitcast(I32),
+            )
+            for b in range(count):
+                rhs[(g, first + b)] = wt[:, b * BANK * 4 : (b + 1) * BANK * 4]
+
+        for g in range(WHOLE):
+            load_words(g, 0, NBANKS)
+        for first, count in PIECES:
+            for g in range(WHOLE, PASSES):
+                load_words(g, first, count)
 
         grouped = keep.tile([P, K], BF16, name="grouped", align_bytes=64)
         xq = keep.tile([P, PASSES * P], U32, name="xq", align_bytes=64)
@@ -107,21 +109,24 @@ def tile_patch_expanding_w_kernel(tc, x, w_words, w_scales, out):
                 out=acc[j][:],
                 lhsT=xq[:, P * g : P * (g + 1)].bitcast(FP8X4),
                 lhsT_scale=xs[:, P * g : P * (g + 1)],
-                rhs=pieces[g][j].bitcast(FP8X4),
+                rhs=rhs[(g, j)].bitcast(FP8X4),
                 rhs_scale=planes[k:P, g // 4, BANK * j : BANK * (j + 1)],
                 start=(g == 0),
                 stop=(g == PASSES - 1),
             )
 
-        for g in range(PASSES - 1):
+        for g in range(WHOLE):
             for j in range(NBANKS):
                 one_pass(g, j)
+        for first, count in PIECES:
+            for g in range(WHOLE, PASSES):
+                for j in range(first, first + count):
+                    one_pass(g, j)
 
-        for first, count in LAST:
+        for first, count in STORES:
             res = keep.tile([P, count * BANK], F32, name="res%d" % first)
             for b in range(count):
                 j = first + b
-                one_pass(PASSES - 1, j)
                 if j % 2 == 0:
                     nc.vector.tensor_copy(out=res[:, BANK * b : BANK * (b + 1)], in_=acc[j][:])
                 else:

@@ -43,11 +43,12 @@ def tile_patch_expanding_w_kernel(tc, x, w_words, w_scales, out):
             in_=ident[:].rearrange("p (i j r) -> p i r j", i=8, j=8, r=2),
         )
 
-        for h in range(2):
-            for q in range(4):
-                nc.sync.dma_start(
-                    out=planes[32 * q : 32 * q + 16, h, :].bitcast(I32),
-                    in_=w_scales[4 * h : 4 * h + 4, 4 * q : 4 * q + 4, :].bitcast(I32),
+        by_plane = w_scales.rearrange("(h a) q n -> a q h n", a=4)
+        for r in range(4):
+            for q in (0, 2, 3, 1):
+                nc.gpsimd.dma_start(
+                    out=planes[32 * q + r : 32 * q + 16 : 4, :, :].bitcast(F32),
+                    in_=by_plane[:, 4 * q + r, :, :].bitcast(F32),
                 )
 
         rhs = {}

@@ -43,13 +43,16 @@ def tile_patch_expanding_w_kernel(tc, x, w_words, w_scales, out):
             in_=ident[:].rearrange("p (i j r) -> p i r j", i=8, j=8, r=2),
         )
 
-        by_plane = w_scales.rearrange("(h a) q n -> a q h n", a=4)
-        for r in range(4):
-            for q in (0, 2, 3, 1):
-                nc.gpsimd.dma_start(
-                    out=planes[32 * q + r : 32 * q + 16 : 4, :, :].bitcast(F32),
-                    in_=by_plane[:, 4 * q + r, :, :].bitcast(F32),
-                )
+        for q in range(4):
+            nc.sync.dma_start(
+                out=planes[32 * q : 32 * q + 16, 0, :].bitcast(I32),
+                in_=w_scales[0:4, 4 * q : 4 * q + 4, :].bitcast(I32),
+            )
+        for q in (0, 2, 3, 1):
+            nc.gpsimd.dma_start(
+                out=planes[32 * q : 32 * q + 16, 1, :].bitcast(F32),
+                in_=w_scales[4:8, 4 * q : 4 * q + 4, :].bitcast(F32),
+            )
 
         rhs = {}
 

@@ -43,17 +43,6 @@ def tile_patch_expanding_w_kernel(tc, x, w_words, w_scales, out):
             in_=ident[:].rearrange("p (i j r) -> p i r j", i=8, j=8, r=2),
         )
 
-        for q in range(4):
-            nc.sync.dma_start(
-                out=planes[32 * q : 32 * q + 16, 0, :].bitcast(I32),
-                in_=w_scales[0:4, 4 * q : 4 * q + 4, :].bitcast(I32),
-            )
-        for q in (0, 2, 3, 1):
-            nc.gpsimd.dma_start(
-                out=planes[32 * q : 32 * q + 16, 1, :].bitcast(F32),
-                in_=w_scales[4:8, 4 * q : 4 * q + 4, :].bitcast(F32),
-            )
-
         rhs = {}
 
         def load_words(g, first, count):
@@ -68,7 +57,14 @@ def tile_patch_expanding_w_kernel(tc, x, w_words, w_scales, out):
             for b in range(count):
                 rhs[(g, first + b)] = wt[:, b * BANK * 4 : (b + 1) * BANK * 4]
 
-        for g in range(WHOLE):
+        load_words(0, 0, NBANKS)
+        for h in range(2):
+            for q in range(4):
+                nc.sync.dma_start(
+                    out=planes[32 * q : 32 * q + 16, h, :].bitcast(I32),
+                    in_=w_scales[4 * h : 4 * h + 4, 4 * q : 4 * q + 4, :].bitcast(I32),
+                )
+        for g in range(1, WHOLE):
             load_words(g, 0, NBANKS)
         for first, count in PIECES:
             for g in range(WHOLE, PASSES):

@@ -29,11 +29,19 @@ def tile_patch_expanding_w_kernel(tc, x, w_words, w_scales, out):
     with tc.tile_pool(name="keep", bufs=1) as keep, tc.psum_pool(
         name="banks", bufs=1
     ) as banks, tc.manual_schedule():
+        planes0 = keep.tile([P, N], U8, name="planes0", align_bytes=64)
+        for q in range(4):
+            nc.sync.dma_start(
+                out=planes0[32 * q : 32 * q + 32, :].bitcast(I32),
+                in_=w_scales[:, 4 * q : 4 * q + 4, :].bitcast(I32),
+            )
+
         x_sb = keep.tile([P, K], BF16, name="x_sb", align_bytes=64)
         nc.sync.dma_start(out=x_sb[:], in_=x_rows)
 
-        planes = keep.tile([P, 2, N], U8, name="planes", align_bytes=64)
-        nc.vector.memset(planes[:].rearrange("p h n -> p (h n)").bitcast(I32), 0)
+        planes1 = keep.tile([P, N], U8, name="planes1", align_bytes=64)
+        nc.vector.memset(planes1[:].bitcast(I32), 0)
+        planes = [planes0, planes1]
 
         ident = keep.tile([P, P], F32, name="ident")
         make_identity(nc, ident[:])
@@ -42,6 +50,12 @@ def tile_patch_expanding_w_kernel(tc, x, w_words, w_scales, out):
             out=perm[:].rearrange("p (i r j) -> p i r j", i=8, r=2, j=8),
             in_=ident[:].rearrange("p (i j r) -> p i r j", i=8, j=8, r=2),
         )
+
+        for q in (0, 2, 3, 1):
+            nc.gpsimd.dma_start(
+                out=planes1[32 * q : 32 * q + 16, :].bitcast(F32),
+                in_=w_scales[4:8, 4 * q : 4 * q + 4, :].bitcast(F32),
+            )
 
         rhs = {}
 
@@ -57,14 +71,7 @@ def tile_patch_expanding_w_kernel(tc, x, w_words, w_scales, out):
             for b in range(count):
                 rhs[(g, first + b)] = wt[:, b * BANK * 4 : (b + 1) * BANK * 4]
 
-        load_words(0, 0, NBANKS)
-        for h in range(2):
-            for q in range(4):
-                nc.sync.dma_start(
-                    out=planes[32 * q : 32 * q + 16, h, :].bitcast(I32),
-                    in_=w_scales[4 * h : 4 * h + 4, 4 * q : 4 * q + 4, :].bitcast(I32),
-                )
-        for g in range(1, WHOLE):
+        for g in range(WHOLE):
             load_words(g, 0, NBANKS)
         for first, count in PIECES:
             for g in range(WHOLE, PASSES):
@@ -110,7 +117,7 @@ def tile_patch_expanding_w_kernel(tc, x, w_words, w_scales, out):
                 lhsT=xq[:, P * g : P * (g + 1)].bitcast(FP8X4),
                 lhsT_scale=xs[:, P * g : P * (g + 1)],
                 rhs=rhs[(g, j)].bitcast(FP8X4),
-                rhs_scale=planes[k:P, g // 4, BANK * j : BANK * (j + 1)],
+                rhs_scale=planes[g // 4][k:P, BANK * j : BANK * (j + 1)],
                 start=(g == 0),
                 stop=(g == PASSES - 1),
             )

import concourse.mybir as mybir
from concourse.masks import make_identity

F32 = mybir.dt.float32
BF16 = mybir.dt.bfloat16
I32 = mybir.dt.int32
U32 = mybir.dt.uint32
U8 = mybir.dt.uint8
FP8X4 = mybir.dt.float8_e4m3fn_x4

P = 128
K = 4096
N = 4096
PASSES = K // 512
BANK = 512
NBANKS = N // BANK
FLOPS = 2 * P * K * N

WHOLE = PASSES - 2
PIECES = [(0, 4), (4, 2), (6, 1), (7, 1)]
STORES = [(0, 2), (2, 2), (4, 2), (6, 1), (7, 1)]


def tile_patch_expanding_w_kernel(tc, x, w_words, w_scales, out):
    nc = tc.nc
    x_rows = x.rearrange("b t (r k) -> (b t r) k", r=2)
    out_rows = out.rearrange("b m n -> (b m) n")

    with tc.tile_pool(name="keep", bufs=1) as keep, tc.psum_pool(
        name="banks", bufs=1
    ) as banks, tc.manual_schedule():
        planes0 = keep.tile([P, N], U8, name="planes0", align_bytes=64)
        for q in range(4):
            nc.sync.dma_start(
                out=planes0[32 * q : 32 * q + 32, :].bitcast(I32),
                in_=w_scales[:, 4 * q : 4 * q + 4, :].bitcast(I32),
            )

        x_sb = keep.tile([P, K], BF16, name="x_sb", align_bytes=64)
        nc.sync.dma_start(out=x_sb[:], in_=x_rows)

        planes1 = keep.tile([P, N], U8, name="planes1", align_bytes=64)
        nc.vector.memset(planes1[:].bitcast(I32), 0)
        planes = [planes0, planes1]

        ident = keep.tile([P, P], F32, name="ident")
        make_identity(nc, ident[:])
        perm = keep.tile([P, P], F32, name="perm")
        nc.vector.tensor_copy(
            out=perm[:].rearrange("p (i r j) -> p i r j", i=8, r=2, j=8),
            in_=ident[:].rearrange("p (i j r) -> p i r j", i=8, j=8, r=2),
        )

        for q in (0, 2, 3, 1):
            nc.gpsimd.dma_start(
                out=planes1[32 * q : 32 * q + 16, :].bitcast(F32),
                in_=w_scales[4:8, 4 * q : 4 * q + 4, :].bitcast(F32),
            )

        rhs = {}

        def load_words(g, first, count):
            wt = keep.tile(
                [P, count * BANK * 4], U8, name="w%d_%d" % (g, first), align_bytes=64
            )
            flat = w_words[g].rearrange("p n t -> p (n t)")
            nc.sync.dma_start(
                out=wt[:].bitcast(I32),
                in_=flat[:, first * BANK * 4 : (first + count) * BANK * 4].bitcast(I32),
            )
            for b in range(count):
                rhs[(g, first + b)] = wt[:, b * BANK * 4 : (b + 1) * BANK * 4]

        for g in range(WHOLE):
            load_words(g, 0, NBANKS)
        for first, count in PIECES:
            for g in range(WHOLE, PASSES):
                load_words(g, first, count)

        grouped = keep.tile([P, K], BF16, name="grouped", align_bytes=64)
        xq = keep.tile([P, PASSES * P], U32, name="xq", align_bytes=64)
        xs = keep.tile([P, PASSES * P], U8, name="xs", align_bytes=64)
        xw = x_sb[:].bitcast(F32)
        gw = grouped[:].bitcast(F32)
        for b in range(4):
            tp = banks.tile([P, 4, P], F32, name="tp%d" % b, tag="bank%d" % b)
            for s in range(4):
                g = 2 * b + s // 2
                u = s % 2
                nc.tensor.transpose(
                    tp[:, s, :], xw[:, 256 * g + u : 256 * (g + 1) : 2], perm[:]
                )
            dst = gw[:, 512 * b : 512 * (b + 1)].rearrange(
                "p (gl m u) -> p gl m u", gl=2, m=P, u=2
            )
            src = tp[:].rearrange("p (gl u) m -> p gl m u", gl=2, u=2)
            if b % 2 == 0:
                nc.vector.tensor_copy(out=dst, in_=src)
            else:
                nc.scalar.copy(out=dst, in_=src)
        for hh in range(2):
            nc.vector.quantize_mx(
                out=xq[:, 512 * hh : 512 * (hh + 1)].bitcast(FP8X4),
                scales=xs[:, 512 * hh : 512 * (hh + 1)],
                in_=grouped[:, 2048 * hh : 2048 * (hh + 1)],
            )

        acc = []
        for j in range(NBANKS):
            acc_j = banks.tile([P, BANK], F32, name="acc%d" % j, tag="bank%d" % j)
            acc.append(acc_j)

        def one_pass(g, j):
            k = 4 * (g % 4)
            nc.tensor.matmul_mx(
                out=acc[j][:],
                lhsT=xq[:, P * g : P * (g + 1)].bitcast(FP8X4),
                lhsT_scale=xs[:, P * g : P * (g + 1)],
                rhs=rhs[(g, j)].bitcast(FP8X4),
                rhs_scale=planes[g // 4][k:P, BANK * j : BANK * (j + 1)],
                start=(g == 0),
                stop=(g == PASSES - 1),
            )

        for g in range(WHOLE):
            for j in range(NBANKS):
                one_pass(g, j)
        for first, count in PIECES:
            for g in range(WHOLE, PASSES):
                for j in range(first, first + count):
                    one_pass(g, j)

        for first, count in STORES:
            res = keep.tile([P, count * BANK], F32, name="res%d" % first)
            for b in range(count):
                j = first + b
                if j % 2 == 0:
                    nc.vector.tensor_copy(out=res[:, BANK * b : BANK * (b + 1)], in_=acc[j][:])
                else:
                    nc.scalar.copy(out=res[:, BANK * b : BANK * (b + 1)], in_=acc[j][:])
            nc.sync.dma_start(
                out=out_rows[:, BANK * first : BANK * (first + count)], in_=res[:]
            )
